import numpy as np
import ml_dtypes


def mxq(x, axis, fmt="e4m3"):
    dtype, down = {"e4m3": (ml_dtypes.float8_e4m3fn, 7), "e5m2": (ml_dtypes.float8_e5m2, 14)}[fmt]
    v = np.moveaxis(np.asarray(x, np.float32).astype(ml_dtypes.bfloat16).astype(np.float64), axis, -1)
    blocks = v.reshape(v.shape[:-1] + (-1, 32))
    amax = np.abs(blocks).max(-1, keepdims=True)
    byte = np.maximum(np.where(amax > 0, np.frexp(amax)[1] - 1 + 127, 0) - down, 1)
    scale = np.exp2(byte - 127.0)
    codes = (blocks / scale).astype(np.float32).astype(dtype).astype(np.float64)
    return np.moveaxis((codes * scale).reshape(v.shape), -1, axis)


WIDE = False


def mx_kscale(k):
    if not WIDE:
        return np.ones(k)
    levels = np.array([10, -10, 5, -5, 0])
    a = np.random.permutation(np.resize(levels, k // 512 * 4)).reshape(k // 512, 4)
    idx = np.arange(k)
    return np.exp2(a[idx // 512, idx % 128 // 32])


BF16 = ml_dtypes.bfloat16


def bf(x):
    return np.asarray(x, np.float32).astype(BF16)


def f64(x):
    return np.asarray(x).astype(np.float64)


B, LQ, LS, D, SIM = 8, 128, 512, 1024, 1024
EPS = 1e-08


def l2norm(x):
    return x / (np.sqrt(np.sum(x * x, axis=-1, keepdims=True)) + EPS)


def setup_inputs():
    s = mx_kscale(D)
    return {"query": bf(np.random.standard_normal((B, LQ, D)) * 0.125 / s),
            "context": bf(np.random.standard_normal((B, LS, D)) * 2.0 * s),
            "matrix": bf(np.random.uniform(size=(B, LQ, D))),
            "smooth": 9}


def reference(query, context, matrix, smooth):
    c = f64(context)
    q = f64(query) * f64(matrix)
    attn = mxq(c, 2, "e4m3") @ mxq(q, 2, "e4m3").transpose(0, 2, 1)
    attn = np.where(attn >= 0, attn, 0.1 * attn)
    attn = l2norm(attn)
    z = attn.transpose(0, 2, 1) * smooth
    e = np.exp(z - z.max(-1, keepdims=True))
    p = e / e.sum(-1, keepdims=True)
    return mxq(p, 2, "e4m3") @ mxq(c, 1, "e4m3")

@@ -1,0 +1,277 @@
+from contextlib import ExitStack
+
+import concourse.mybir as mybir
+from concourse.masks import make_identity
+
+FP8X4 = mybir.dt.float8_e4m3fn_x4
+BF16 = mybir.dt.bfloat16
+F32 = mybir.dt.float32
+U32 = mybir.dt.uint32
+U8 = mybir.dt.uint8
+ACT = mybir.ActivationFunctionType
+ALU = mybir.AluOpType
+
+B, LQ, LS, D = 8, 128, 512, 1024
+EPS = 1e-08
+NEGATIVE_SLOPE = 0.1
+P = 128
+PACK = 4
+K_PASS = P * PACK
+D_PASSES = D // K_PASS
+N_MAX = 512
+D_HALVES = D // N_MAX
+FLOPS = 2 * 2 * B * LS * LQ * D
+
+
+def tile_alignment_vector_pa_kernel(tc, query, context, matrix, smooth, out):
+    nc = tc.nc
+    assert smooth > 0
+    with ExitStack() as ctx:
+        const = ctx.enter_context(tc.tile_pool(name="const", bufs=1))
+        inputs = ctx.enter_context(tc.tile_pool(name="inputs", bufs=B))
+        pair = ctx.enter_context(tc.tile_pool(name="pair", bufs=2))
+        kept = ctx.enter_context(tc.tile_pool(name="kept", bufs=4))
+        flip_psum = ctx.enter_context(tc.psum_pool(name="flip_psum", bufs=4))
+        one_psum = ctx.enter_context(tc.psum_pool(name="one_psum", bufs=1))
+
+        ident_f32 = const.tile([P, P], F32)
+        make_identity(nc, ident_f32[:])
+        ident_bf16 = const.tile([P, P], BF16)
+        make_identity(nc, ident_bf16[:])
+        ones = const.tile([P, 1], F32)
+        nc.vector.memset(ones[:], 1.0)
+        half = const.tile([P, PACK], F32)
+        nc.vector.memset(half[:], 0.5)
+        warm = const.tile([P, 1], F32)
+        nc.scalar.activation(out=warm[:], in_=ones[:], func=ACT.Exp)
+
+        query_sb, matrix_sb, c_sb = {}, {}, {}
+        q_sb, q_grouped, q_codes, q_scales = {}, {}, {}, {}
+        ct_grouped, ct_codes, ct_scales = {}, {}, {}
+        c_grouped, c_codes, c_scales = {}, {}, {}
+        scores_ps, lrelu, norms, exp_scale, weights, sums_ps, sum_recip = {}, {}, {}, {}, {}, {}, {}
+        p_grouped, p_codes, p_scales, out_ps = {}, {}, {}, {}
+
+        def load(n):
+            query_tile = inputs.tile([P, D], BF16)
+            nc.sync.dma_start(out=query_tile[:], in_=query[n])
+            matrix_tile = inputs.tile([P, D], BF16)
+            nc.sync.dma_start(out=matrix_tile[:], in_=matrix[n])
+            c_tile = inputs.tile([P, PACK, D], BF16)
+            nc.sync.dma_start(out=c_tile[:], in_=context[n].rearrange("(p t) d -> p t d", t=PACK))
+            query_sb[n], matrix_sb[n], c_sb[n] = query_tile, matrix_tile, c_tile
+
+        def gate_queries(n):
+            q_tile = pair.tile([P, D], BF16)
+            nc.vector.tensor_tensor(out=q_tile[:], in0=query_sb[n][:], in1=matrix_sb[n][:], op=ALU.mult)
+            q_sb[n] = q_tile
+
+        def transpose_queries(n):
+            by_parity = q_sb[n][:].rearrange("j (k r e) -> j k e r", r=P, e=2)
+            qt_ps = flip_psum.tile([P, D_PASSES * PACK, LQ], BF16, tag="flip")
+            for k in range(D // (2 * P)):
+                for e in range(2):
+                    nc.tensor.transpose(qt_ps[:, 2 * k + e, :], by_parity[:, k, e, :], ident_bf16[:])
+            grouped = pair.tile([P, D_PASSES * LQ * PACK], BF16, align_bytes=64, name="q_grouped")
+            nc.scalar.copy(
+                out=grouped[:].rearrange("r (g j v) -> r g j v", g=D_PASSES, v=PACK),
+                in_=qt_ps[:].rearrange("r (g v) j -> r g j v", g=D_PASSES),
+            )
+            q_grouped[n] = grouped
+
+        def transpose_sources(n, g):
+            grouped = pair.tile([P, PACK * P * PACK], BF16, align_bytes=64, name="ct_grouped%d" % g)
+            grouped_words = grouped[:].bitcast(F32)
+            for t_pair in range(PACK // 2):
+                ct_ps = flip_psum.tile([P, 2, 2, P], F32, tag="flip")
+                for x in range(2):
+                    c_words = c_sb[n][:, 2 * t_pair + x, :].bitcast(F32)
+                    for u in range(2):
+                        k = 2 * g + u
+                        nc.tensor.transpose(ct_ps[:, x, u, :], c_words[:, k * P : (k + 1) * P], ident_f32[:])
+                nc.scalar.copy(
+                    out=grouped_words[:, t_pair * N_MAX : (t_pair + 1) * N_MAX].rearrange(
+                        "r (x p u) -> r x p u", x=2, u=2
+                    ),
+                    in_=ct_ps[:].rearrange("r x u p -> r x p u"),
+                )
+            ct_grouped[n, g] = grouped
+
+        def quantise_queries(n):
+            codes = pair.tile([P, D_PASSES * LQ], U32, align_bytes=64, name="q_codes")
+            scales = pair.tile([P, D_PASSES * LQ], U8, align_bytes=64, name="q_scales")
+            nc.vector.quantize_mx(out=codes[:].bitcast(FP8X4), scales=scales[:], in_=q_grouped[n][:])
+            q_codes[n], q_scales[n] = codes, scales
+
+        def quantise_features(n, g):
+            codes = pair.tile([P, PACK * P], U32, align_bytes=64, name="ct_codes%d" % g)
+            scales = pair.tile([P, PACK * P], U8, align_bytes=64, name="ct_scales%d" % g)
+            nc.vector.quantize_mx(out=codes[:].bitcast(FP8X4), scales=scales[:], in_=ct_grouped[n, g][:])
+            ct_codes[n, g], ct_scales[n, g] = codes, scales
+
+        def regroup_sources(n, h):
+            grouped = pair.tile([P, N_MAX, PACK], BF16, align_bytes=64, name="c_grouped%d" % h)
+            nc.vector.tensor_copy(
+                out=grouped[:].rearrange("p (c i) t -> p c t i", i=4),
+                in_=c_sb[n][:, :, h * N_MAX : (h + 1) * N_MAX].rearrange("p t (c i) -> p c t i", i=4),
+            )
+            c_grouped[n, h] = grouped
+
+        def quantise_sources(n, h):
+            codes = kept.tile([P, N_MAX], U32, align_bytes=64, name="c_codes%d" % h)
+            scales = kept.tile([P, N_MAX], U8, align_bytes=64, name="c_scales%d" % h)
+            nc.vector.quantize_mx(
+                out=codes[:].bitcast(FP8X4), scales=scales[:], in_=c_grouped[n, h][:].rearrange("p d t -> p (d t)")
+            )
+            c_codes[n, h], c_scales[n, h] = codes, scales
+
+        def score_matmul(n):
+            a_ps = one_psum.tile([P, PACK, LQ], F32, name="scores_ps")
+            for t in range(PACK):
+                for g in range(D_PASSES):
+                    s_cols = slice(t * P, (t + 1) * P)
+                    j_cols = slice(g * LQ, (g + 1) * LQ)
+                    nc.tensor.matmul_mx(
+                        out=a_ps[:, t, :],
+                        lhsT=ct_codes[n, g][:, s_cols].bitcast(FP8X4),
+                        lhsT_scale=ct_scales[n, g][:, s_cols],
+                        rhs=q_codes[n][:, j_cols].bitcast(FP8X4),
+                        rhs_scale=q_scales[n][:, j_cols],
+                        start=(g == 0),
+                        stop=(g == D_PASSES - 1),
+                    )
+            scores_ps[n] = a_ps
+
+        def leaky_relu(n):
+            a_sb = pair.tile([P, PACK, LQ], F32)
+            nc.scalar.copy(out=a_sb[:], in_=scores_ps[n][:])
+            l_sb = pair.tile([P, PACK, LQ], F32)
+            nc.vector.scalar_tensor_tensor(
+                out=l_sb[:], in0=a_sb[:], scalar=NEGATIVE_SLOPE, in1=a_sb[:], op0=ALU.mult, op1=ALU.max
+            )
+            lrelu[n] = l_sb
+
+        def norm_over_queries(n):
+            squares = pair.tile([P, LQ], F32)
+            square_sum = pair.tile([P, PACK], F32)
+            for t in range(PACK):
+                nc.scalar.activation(
+                    out=squares[:],
+                    in_=lrelu[n][:, t, :],
+                    func=ACT.Square,
+                    scale=1.0 / smooth,
+                    accum_out=square_sum[:, t : t + 1],
+                )
+            root = pair.tile([P, PACK], F32)
+            nc.gpsimd.tensor_tensor(out=root[:], in0=square_sum[:], in1=half[:], op=ALU.pow)
+            norm = pair.tile([P, PACK], F32)
+            nc.gpsimd.tensor_scalar(out=norm[:], in0=root[:], scalar1=EPS / smooth, scalar2=None, op0=ALU.add)
+            norms[n] = norm
+
+        def invert_norm(n):
+            scale = pair.tile([P, PACK], F32)
+            nc.vector.reciprocal(out=scale[:], in_=norms[n][:])
+            exp_scale[n] = scale
+
+        def exponentials(n):
+            e_sb = pair.tile([P, PACK, LQ], F32)
+            for t in range(PACK):
+                nc.scalar.activation(
+                    out=e_sb[:, t, :],
+                    in_=lrelu[n][:, t, :],
+                    func=ACT.Exp,
+                    bias=-float(smooth),
+                    scale=exp_scale[n][:, t : t + 1],
+                )
+            weights[n] = e_sb
+
+        def sum_over_sources(n):
+            s_ps = one_psum.tile([P, LQ + 1], F32, name="sums_ps")
+            for t in range(PACK):
+                nc.tensor.matmul(
+                    out=s_ps[:, LQ : LQ + 1], lhsT=weights[n][:, t, :], rhs=ones[:], start=(t == 0), stop=(t == PACK - 1)
+                )
+            sums_ps[n] = s_ps
+
+        def invert_sums(n):
+            recip = pair.tile([P, 1], F32)
+            nc.vector.reciprocal(out=recip[:], in_=sums_ps[n][:, LQ : LQ + 1])
+            sum_recip[n] = recip
+
+        def spread_sums(n):
+            nc.tensor.matmul(
+                out=sums_ps[n][:, 0:LQ],
+                lhsT=sum_recip[n][:, 0:1].to_broadcast([P, P]),
+                rhs=ident_f32[:],
+                start=True,
+                stop=True,
+            )
+
+        def normalise_weights(n):
+            grouped = pair.tile([P, LQ * PACK], BF16, align_bytes=64, name="p_grouped")
+            nc.vector.tensor_tensor(
+                out=grouped[:].rearrange("p (j t) -> p j t", t=PACK),
+                in0=weights[n][:].rearrange("p t j -> p j t"),
+                in1=sums_ps[n][:, 0:LQ].unsqueeze(2).to_broadcast([P, LQ, PACK]),
+                op=ALU.mult,
+            )
+            p_grouped[n] = grouped
+
+        def quantise_weights(n):
+            codes = pair.tile([P, LQ], U32, align_bytes=64, name="p_codes")
+            scales = pair.tile([P, LQ], U8, align_bytes=64, name="p_scales")
+            nc.vector.quantize_mx(out=codes[:].bitcast(FP8X4), scales=scales[:], in_=p_grouped[n][:])
+            p_codes[n], p_scales[n] = codes, scales
+
+        def weighted_sum(n):
+            for h in range(D_HALVES):
+                o_ps = one_psum.tile([P, N_MAX], F32, name="out_ps%d" % h)
+                nc.tensor.matmul_mx(
+                    out=o_ps[:],
+                    lhsT=p_codes[n][:].bitcast(FP8X4),
+                    lhsT_scale=p_scales[n][:],
+                    rhs=c_codes[n, h][:].bitcast(FP8X4),
+                    rhs_scale=c_scales[n, h][:],
+                    start=True,
+                    stop=True,
+                )
+                out_ps[n, h] = o_ps
+
+        def store_result(n):
+            for h in range(D_HALVES):
+                out_sb = pair.tile([P, N_MAX], F32, name="out_sb%d" % h)
+                nc.scalar.copy(out=out_sb[:], in_=out_ps[n, h][:])
+                nc.sync.dma_start(out=out[n][:, h * N_MAX : (h + 1) * N_MAX], in_=out_sb[:])
+
+        def run(stage, n, *more):
+            if 0 <= n < B:
+                stage(n, *more)
+
+        ctx.enter_context(tc.manual_schedule())
+        for n in range(B):
+            load(n)
+        gate_queries(0)
+        for i in range(B + 3):
+            run(invert_sums, i - 3)
+            run(spread_sums, i - 3)
+            run(norm_over_queries, i - 2)
+            run(quantise_queries, i - 1)
+            run(normalise_weights, i - 3)
+            run(transpose_queries, i)
+            run(transpose_sources, i, 0)
+            run(quantise_features, i - 1, 0)
+            run(quantise_weights, i - 3)
+            run(quantise_features, i - 1, 1)
+            run(regroup_sources, i, 0)
+            run(invert_norm, i - 2)
+            run(quantise_sources, i, 0)
+            run(regroup_sources, i - 2, 1)
+            run(weighted_sum, i - 3)
+            run(score_matmul, i - 1)
+            run(leaky_relu, i - 1)
+            run(exponentials, i - 2)
+            run(transpose_sources, i, 1)
+            run(quantise_sources, i - 2, 1)
+            run(store_result, i - 3)
+            run(sum_over_sources, i - 2)
+            run(gate_queries, i + 1)

@@ -20,6 +20,7 @@ K_PASS = P * PACK
 D_PASSES = D // K_PASS
 N_MAX = 512
 D_HALVES = D // N_MAX
+STEPS_1 = B + 1
 FLOPS = 2 * 2 * B * LS * LQ * D
 
 
@@ -28,11 +29,11 @@ def tile_alignment_vector_pa_kernel(tc, query, context, matrix, smooth, out):
     assert smooth > 0
     with ExitStack() as ctx:
         const = ctx.enter_context(tc.tile_pool(name="const", bufs=1))
-        inputs = ctx.enter_context(tc.tile_pool(name="inputs", bufs=B))
+        whole = ctx.enter_context(tc.tile_pool(name="whole", bufs=B))
+        gates = ctx.enter_context(tc.tile_pool(name="gates", bufs=4))
         pair = ctx.enter_context(tc.tile_pool(name="pair", bufs=2))
-        kept = ctx.enter_context(tc.tile_pool(name="kept", bufs=4))
-        flip_psum = ctx.enter_context(tc.psum_pool(name="flip_psum", bufs=4))
-        one_psum = ctx.enter_context(tc.psum_pool(name="one_psum", bufs=1))
+        four_psum = ctx.enter_context(tc.psum_pool(name="four_psum", bufs=4))
+        two_psum = ctx.enter_context(tc.psum_pool(name="two_psum", bufs=2))
 
         ident_f32 = const.tile([P, P], F32)
         make_identity(nc, ident_f32[:])
@@ -40,24 +41,24 @@ def tile_alignment_vector_pa_kernel(tc, query, context, matrix, smooth, out):
         make_identity(nc, ident_bf16[:])
         ones = const.tile([P, 1], F32)
         nc.vector.memset(ones[:], 1.0)
-        half = const.tile([P, PACK], F32)
-        nc.vector.memset(half[:], 0.5)
         warm = const.tile([P, 1], F32)
-        nc.scalar.activation(out=warm[:], in_=ones[:], func=ACT.Exp)
+        nc.scalar.activation(out=warm[:], in_=ones[:], func=ACT.Sqrt)
+        square_sums = const.tile([P, B, PACK], F32)
+        exp_scales = const.tile([P, B, PACK], F32)
 
         query_sb, matrix_sb, c_sb = {}, {}, {}
         q_sb, q_grouped, q_codes, q_scales = {}, {}, {}, {}
         ct_grouped, ct_codes, ct_scales = {}, {}, {}
         c_grouped, c_codes, c_scales = {}, {}, {}
-        scores_ps, lrelu, norms, exp_scale, weights, sums_ps, sum_recip = {}, {}, {}, {}, {}, {}, {}
+        scores_ps, lrelu, weights, sums_ps, sum_recip = {}, {}, {}, {}, {}
         p_grouped, p_codes, p_scales, out_ps = {}, {}, {}, {}
 
         def load(n):
-            query_tile = inputs.tile([P, D], BF16)
+            query_tile = gates.tile([P, D], BF16)
             nc.sync.dma_start(out=query_tile[:], in_=query[n])
-            matrix_tile = inputs.tile([P, D], BF16)
+            matrix_tile = gates.tile([P, D], BF16)
             nc.sync.dma_start(out=matrix_tile[:], in_=matrix[n])
-            c_tile = inputs.tile([P, PACK, D], BF16)
+            c_tile = whole.tile([P, PACK, D], BF16)
             nc.sync.dma_start(out=c_tile[:], in_=context[n].rearrange("(p t) d -> p t d", t=PACK))
             query_sb[n], matrix_sb[n], c_sb[n] = query_tile, matrix_tile, c_tile
 
@@ -68,7 +69,7 @@ def tile_alignment_vector_pa_kernel(tc, query, context, matrix, smooth, out):
 
         def transpose_queries(n):
             by_parity = q_sb[n][:].rearrange("j (k r e) -> j k e r", r=P, e=2)
-            qt_ps = flip_psum.tile([P, D_PASSES * PACK, LQ], BF16, tag="flip")
+            qt_ps = four_psum.tile([P, D_PASSES * PACK, LQ], BF16, tag="bank")
             for k in range(D // (2 * P)):
                 for e in range(2):
                     nc.tensor.transpose(qt_ps[:, 2 * k + e, :], by_parity[:, k, e, :], ident_bf16[:])
@@ -83,7 +84,7 @@ def tile_alignment_vector_pa_kernel(tc, query, context, matrix, smooth, out):
             grouped = pair.tile([P, PACK * P * PACK], BF16, align_bytes=64, name="ct_grouped%d" % g)
             grouped_words = grouped[:].bitcast(F32)
             for t_pair in range(PACK // 2):
-                ct_ps = flip_psum.tile([P, 2, 2, P], F32, tag="flip")
+                ct_ps = four_psum.tile([P, 2, 2, P], F32, tag="bank")
                 for x in range(2):
                     c_words = c_sb[n][:, 2 * t_pair + x, :].bitcast(F32)
                     for u in range(2):
@@ -109,24 +110,25 @@ def tile_alignment_vector_pa_kernel(tc, query, context, matrix, smooth, out):
             nc.vector.quantize_mx(out=codes[:].bitcast(FP8X4), scales=scales[:], in_=ct_grouped[n, g][:])
             ct_codes[n, g], ct_scales[n, g] = codes, scales
 
-        def regroup_sources(n, h):
-            grouped = pair.tile([P, N_MAX, PACK], BF16, align_bytes=64, name="c_grouped%d" % h)
+        def regroup_sources(half):
+            n, h = divmod(half, D_HALVES)
+            grouped = pair.tile([P, N_MAX, PACK], BF16, align_bytes=64, name="c_grouped")
             nc.vector.tensor_copy(
                 out=grouped[:].rearrange("p (c i) t -> p c t i", i=4),
                 in_=c_sb[n][:, :, h * N_MAX : (h + 1) * N_MAX].rearrange("p t (c i) -> p c t i", i=4),
             )
-            c_grouped[n, h] = grouped
+            c_grouped[half] = grouped
 
-        def quantise_sources(n, h):
-            codes = kept.tile([P, N_MAX], U32, align_bytes=64, name="c_codes%d" % h)
-            scales = kept.tile([P, N_MAX], U8, align_bytes=64, name="c_scales%d" % h)
+        def quantise_sources(half):
+            codes = whole.tile([P, N_MAX], U32, align_bytes=64, name="c_codes%d" % (half % D_HALVES))
+            scales = whole.tile([P, N_MAX], U8, align_bytes=64, name="c_scales%d" % (half % D_HALVES))
             nc.vector.quantize_mx(
-                out=codes[:].bitcast(FP8X4), scales=scales[:], in_=c_grouped[n, h][:].rearrange("p d t -> p (d t)")
+                out=codes[:].bitcast(FP8X4), scales=scales[:], in_=c_grouped[half][:].rearrange("p d t -> p (d t)")
             )
-            c_codes[n, h], c_scales[n, h] = codes, scales
+            c_codes[half], c_scales[half] = codes, scales
 
         def score_matmul(n):
-            a_ps = one_psum.tile([P, PACK, LQ], F32, name="scores_ps")
+            a_ps = two_psum.tile([P, PACK, LQ], F32, name="scores_ps")
             for t in range(PACK):
                 for g in range(D_PASSES):
                     s_cols = slice(t * P, (t + 1) * P)
@@ -145,33 +147,29 @@ def tile_alignment_vector_pa_kernel(tc, query, context, matrix, smooth, out):
         def leaky_relu(n):
             a_sb = pair.tile([P, PACK, LQ], F32)
             nc.scalar.copy(out=a_sb[:], in_=scores_ps[n][:])
-            l_sb = pair.tile([P, PACK, LQ], F32)
+            l_sb = whole.tile([P, PACK, LQ], F32)
             nc.vector.scalar_tensor_tensor(
                 out=l_sb[:], in0=a_sb[:], scalar=NEGATIVE_SLOPE, in1=a_sb[:], op0=ALU.mult, op1=ALU.max
             )
             lrelu[n] = l_sb
 
-        def norm_over_queries(n):
+        def sum_squares(n):
             squares = pair.tile([P, LQ], F32)
-            square_sum = pair.tile([P, PACK], F32)
             for t in range(PACK):
                 nc.scalar.activation(
                     out=squares[:],
                     in_=lrelu[n][:, t, :],
                     func=ACT.Square,
                     scale=1.0 / smooth,
-                    accum_out=square_sum[:, t : t + 1],
+                    accum_out=square_sums[:, n, t : t + 1],
                 )
-            root = pair.tile([P, PACK], F32)
-            nc.gpsimd.tensor_tensor(out=root[:], in0=square_sum[:], in1=half[:], op=ALU.pow)
-            norm = pair.tile([P, PACK], F32)
-            nc.gpsimd.tensor_scalar(out=norm[:], in0=root[:], scalar1=EPS / smooth, scalar2=None, op0=ALU.add)
-            norms[n] = norm
 
-        def invert_norm(n):
-            scale = pair.tile([P, PACK], F32)
-            nc.vector.reciprocal(out=scale[:], in_=norms[n][:])
-            exp_scale[n] = scale
+        def invert_norms():
+            norms = const.tile([P, B, PACK], F32)
+            nc.scalar.activation(out=norms[:], in_=square_sums[:], func=ACT.Sqrt)
+            padded = const.tile([P, B, PACK], F32)
+            nc.vector.tensor_scalar(out=padded[:], in0=norms[:], scalar1=EPS / smooth, scalar2=None, op0=ALU.add)
+            nc.vector.reciprocal(out=exp_scales[:], in_=padded[:])
 
         def exponentials(n):
             e_sb = pair.tile([P, PACK, LQ], F32)
@@ -181,12 +179,12 @@ def tile_alignment_vector_pa_kernel(tc, query, context, matrix, smooth, out):
                     in_=lrelu[n][:, t, :],
                     func=ACT.Exp,
                     bias=-float(smooth),
-                    scale=exp_scale[n][:, t : t + 1],
+                    scale=exp_scales[:, n, t : t + 1],
                 )
             weights[n] = e_sb
 
         def sum_over_sources(n):
-            s_ps = one_psum.tile([P, LQ + 1], F32, name="sums_ps")
+            s_ps = two_psum.tile([P, LQ + 1], F32, name="sums_ps")
             for t in range(PACK):
                 nc.tensor.matmul(
                     out=s_ps[:, LQ : LQ + 1], lhsT=weights[n][:, t, :], rhs=ones[:], start=(t == 0), stop=(t == PACK - 1)
@@ -225,13 +223,13 @@ def tile_alignment_vector_pa_kernel(tc, query, context, matrix, smooth, out):
 
         def weighted_sum(n):
             for h in range(D_HALVES):
-                o_ps = one_psum.tile([P, N_MAX], F32, name="out_ps%d" % h)
+                o_ps = four_psum.tile([P, N_MAX], F32, tag="bank")
                 nc.tensor.matmul_mx(
                     out=o_ps[:],
                     lhsT=p_codes[n][:].bitcast(FP8X4),
                     lhsT_scale=p_scales[n][:],
-                    rhs=c_codes[n, h][:].bitcast(FP8X4),
-                    rhs_scale=c_scales[n, h][:],
+                    rhs=c_codes[n * D_HALVES + h][:].bitcast(FP8X4),
+                    rhs_scale=c_scales[n * D_HALVES + h][:],
                     start=True,
                     stop=True,
                 )
@@ -247,31 +245,38 @@ def tile_alignment_vector_pa_kernel(tc, query, context, matrix, smooth, out):
             if 0 <= n < B:
                 stage(n, *more)
 
+        def run_half(stage, half):
+            if half < B * D_HALVES:
+                stage(half)
+
         ctx.enter_context(tc.manual_schedule())
         for n in range(B):
             load(n)
         gate_queries(0)
-        for i in range(B + 3):
-            run(invert_sums, i - 3)
-            run(spread_sums, i - 3)
-            run(norm_over_queries, i - 2)
-            run(quantise_queries, i - 1)
-            run(normalise_weights, i - 3)
+
+        for i in range(STEPS_1):
             run(transpose_queries, i)
             run(transpose_sources, i, 0)
+            run(quantise_queries, i - 1)
             run(quantise_features, i - 1, 0)
-            run(quantise_weights, i - 3)
             run(quantise_features, i - 1, 1)
-            run(regroup_sources, i, 0)
-            run(invert_norm, i - 2)
-            run(quantise_sources, i, 0)
-            run(regroup_sources, i - 2, 1)
-            run(weighted_sum, i - 3)
             run(score_matmul, i - 1)
-            run(leaky_relu, i - 1)
-            run(exponentials, i - 2)
-            run(transpose_sources, i, 1)
-            run(quantise_sources, i - 2, 1)
-            run(store_result, i - 3)
-            run(sum_over_sources, i - 2)
+            run_half(regroup_sources, i)
             run(gate_queries, i + 1)
+            run(leaky_relu, i - 1)
+            run(transpose_sources, i, 1)
+            run_half(quantise_sources, i)
+            run(sum_squares, i - 1)
+        invert_norms()
+
+        for k in range(B + 2):
+            run(exponentials, k)
+            run(weighted_sum, k - 2)
+            run(invert_sums, k - 1)
+            run(spread_sums, k - 1)
+            run(sum_over_sources, k)
+            run_half(regroup_sources, STEPS_1 + k)
+            run(normalise_weights, k - 1)
+            run_half(quantise_sources, STEPS_1 + k)
+            run(quantise_weights, k - 1)
+            run(store_result, k - 2)

@@ -20,7 +20,6 @@ K_PASS = P * PACK
 D_PASSES = D // K_PASS
 N_MAX = 512
 D_HALVES = D // N_MAX
-STEPS_1 = B + 1
 FLOPS = 2 * 2 * B * LS * LQ * D
 
 
@@ -29,36 +28,37 @@ def tile_alignment_vector_pa_kernel(tc, query, context, matrix, smooth, out):
     assert smooth > 0
     with ExitStack() as ctx:
         const = ctx.enter_context(tc.tile_pool(name="const", bufs=1))
-        whole = ctx.enter_context(tc.tile_pool(name="whole", bufs=B))
-        gates = ctx.enter_context(tc.tile_pool(name="gates", bufs=4))
+        inputs = ctx.enter_context(tc.tile_pool(name="inputs", bufs=B))
         pair = ctx.enter_context(tc.tile_pool(name="pair", bufs=2))
-        four_psum = ctx.enter_context(tc.psum_pool(name="four_psum", bufs=4))
-        two_psum = ctx.enter_context(tc.psum_pool(name="two_psum", bufs=2))
+        kept = ctx.enter_context(tc.tile_pool(name="kept", bufs=4))
+        whole = ctx.enter_context(tc.tile_pool(name="whole", bufs=B))
+        flip_psum = ctx.enter_context(tc.psum_pool(name="flip_psum", bufs=4))
+        one_psum = ctx.enter_context(tc.psum_pool(name="one_psum", bufs=1))
 
         ident_f32 = const.tile([P, P], F32)
         make_identity(nc, ident_f32[:])
         ident_bf16 = const.tile([P, P], BF16)
         make_identity(nc, ident_bf16[:])
-        ones = const.tile([P, 1], F32)
+        ones = const.tile([P, P], F32)
         nc.vector.memset(ones[:], 1.0)
+        half = const.tile([P, PACK], F32)
+        nc.vector.memset(half[:], 0.5)
         warm = const.tile([P, 1], F32)
-        nc.scalar.activation(out=warm[:], in_=ones[:], func=ACT.Sqrt)
-        square_sums = const.tile([P, B, PACK], F32)
-        exp_scales = const.tile([P, B, PACK], F32)
+        nc.scalar.activation(out=warm[:], in_=ones[:, 0:1], func=ACT.Exp)
 
         query_sb, matrix_sb, c_sb = {}, {}, {}
         q_sb, q_grouped, q_codes, q_scales = {}, {}, {}, {}
         ct_grouped, ct_codes, ct_scales = {}, {}, {}
         c_grouped, c_codes, c_scales = {}, {}, {}
-        scores_ps, lrelu, weights, sums_ps, sum_recip = {}, {}, {}, {}, {}
+        scores_ps, lrelu, norms, exp_scale, weights, sums_ps, sum_recip = {}, {}, {}, {}, {}, {}, {}
         p_grouped, p_codes, p_scales, out_ps = {}, {}, {}, {}
 
         def load(n):
-            query_tile = gates.tile([P, D], BF16)
+            query_tile = inputs.tile([P, D], BF16)
             nc.sync.dma_start(out=query_tile[:], in_=query[n])
-            matrix_tile = gates.tile([P, D], BF16)
+            matrix_tile = inputs.tile([P, D], BF16)
             nc.sync.dma_start(out=matrix_tile[:], in_=matrix[n])
-            c_tile = whole.tile([P, PACK, D], BF16)
+            c_tile = inputs.tile([P, PACK, D], BF16)
             nc.sync.dma_start(out=c_tile[:], in_=context[n].rearrange("(p t) d -> p t d", t=PACK))
             query_sb[n], matrix_sb[n], c_sb[n] = query_tile, matrix_tile, c_tile
 
@@ -69,7 +69,7 @@ def tile_alignment_vector_pa_kernel(tc, query, context, matrix, smooth, out):
 
         def transpose_queries(n):
             by_parity = q_sb[n][:].rearrange("j (k r e) -> j k e r", r=P, e=2)
-            qt_ps = four_psum.tile([P, D_PASSES * PACK, LQ], BF16, tag="bank")
+            qt_ps = flip_psum.tile([P, D_PASSES * PACK, LQ], BF16, tag="flip")
             for k in range(D // (2 * P)):
                 for e in range(2):
                     nc.tensor.transpose(qt_ps[:, 2 * k + e, :], by_parity[:, k, e, :], ident_bf16[:])
@@ -84,7 +84,7 @@ def tile_alignment_vector_pa_kernel(tc, query, context, matrix, smooth, out):
             grouped = pair.tile([P, PACK * P * PACK], BF16, align_bytes=64, name="ct_grouped%d" % g)
             grouped_words = grouped[:].bitcast(F32)
             for t_pair in range(PACK // 2):
-                ct_ps = four_psum.tile([P, 2, 2, P], F32, tag="bank")
+                ct_ps = flip_psum.tile([P, 2, 2, P], F32, tag="flip")
                 for x in range(2):
                     c_words = c_sb[n][:, 2 * t_pair + x, :].bitcast(F32)
                     for u in range(2):
@@ -110,25 +110,24 @@ def tile_alignment_vector_pa_kernel(tc, query, context, matrix, smooth, out):
             nc.vector.quantize_mx(out=codes[:].bitcast(FP8X4), scales=scales[:], in_=ct_grouped[n, g][:])
             ct_codes[n, g], ct_scales[n, g] = codes, scales
 
-        def regroup_sources(half):
-            n, h = divmod(half, D_HALVES)
-            grouped = pair.tile([P, N_MAX, PACK], BF16, align_bytes=64, name="c_grouped")
+        def regroup_sources(n, h):
+            grouped = pair.tile([P, N_MAX, PACK], BF16, align_bytes=64, name="c_grouped%d" % h)
             nc.vector.tensor_copy(
                 out=grouped[:].rearrange("p (c i) t -> p c t i", i=4),
                 in_=c_sb[n][:, :, h * N_MAX : (h + 1) * N_MAX].rearrange("p t (c i) -> p c t i", i=4),
             )
-            c_grouped[half] = grouped
+            c_grouped[n, h] = grouped
 
-        def quantise_sources(half):
-            codes = whole.tile([P, N_MAX], U32, align_bytes=64, name="c_codes%d" % (half % D_HALVES))
-            scales = whole.tile([P, N_MAX], U8, align_bytes=64, name="c_scales%d" % (half % D_HALVES))
+        def quantise_sources(n, h):
+            codes = whole.tile([P, N_MAX], U32, align_bytes=64, name="c_codes%d" % h)
+            scales = whole.tile([P, N_MAX], U8, align_bytes=64, name="c_scales%d" % h)
             nc.vector.quantize_mx(
-                out=codes[:].bitcast(FP8X4), scales=scales[:], in_=c_grouped[half][:].rearrange("p d t -> p (d t)")
+                out=codes[:].bitcast(FP8X4), scales=scales[:], in_=c_grouped[n, h][:].rearrange("p d t -> p (d t)")
             )
-            c_codes[half], c_scales[half] = codes, scales
+            c_codes[n, h], c_scales[n, h] = codes, scales
 
         def score_matmul(n):
-            a_ps = two_psum.tile([P, PACK, LQ], F32, name="scores_ps")
+            a_ps = one_psum.tile([P, PACK, LQ], F32, name="scores_ps")
             for t in range(PACK):
                 for g in range(D_PASSES):
                     s_cols = slice(t * P, (t + 1) * P)
@@ -147,29 +146,33 @@ def tile_alignment_vector_pa_kernel(tc, query, context, matrix, smooth, out):
         def leaky_relu(n):
             a_sb = pair.tile([P, PACK, LQ], F32)
             nc.scalar.copy(out=a_sb[:], in_=scores_ps[n][:])
-            l_sb = whole.tile([P, PACK, LQ], F32)
+            l_sb = kept.tile([P, PACK, LQ], F32)
             nc.vector.scalar_tensor_tensor(
                 out=l_sb[:], in0=a_sb[:], scalar=NEGATIVE_SLOPE, in1=a_sb[:], op0=ALU.mult, op1=ALU.max
             )
             lrelu[n] = l_sb
 
-        def sum_squares(n):
+        def norm_over_queries(n):
             squares = pair.tile([P, LQ], F32)
+            square_sum = pair.tile([P, PACK], F32)
             for t in range(PACK):
                 nc.scalar.activation(
                     out=squares[:],
                     in_=lrelu[n][:, t, :],
                     func=ACT.Square,
                     scale=1.0 / smooth,
-                    accum_out=square_sums[:, n, t : t + 1],
+                    accum_out=square_sum[:, t : t + 1],
                 )
+            root = pair.tile([P, PACK], F32)
+            nc.gpsimd.tensor_tensor(out=root[:], in0=square_sum[:], in1=half[:], op=ALU.pow)
+            norm = pair.tile([P, PACK], F32)
+            nc.gpsimd.tensor_scalar(out=norm[:], in0=root[:], scalar1=EPS / smooth, scalar2=None, op0=ALU.add)
+            norms[n] = norm
 
-        def invert_norms():
-            norms = const.tile([P, B, PACK], F32)
-            nc.scalar.activation(out=norms[:], in_=square_sums[:], func=ACT.Sqrt)
-            padded = const.tile([P, B, PACK], F32)
-            nc.vector.tensor_scalar(out=padded[:], in0=norms[:], scalar1=EPS / smooth, scalar2=None, op0=ALU.add)
-            nc.vector.reciprocal(out=exp_scales[:], in_=padded[:])
+        def invert_norm(n):
+            scale = pair.tile([P, PACK], F32)
+            nc.vector.reciprocal(out=scale[:], in_=norms[n][:])
+            exp_scale[n] = scale
 
         def exponentials(n):
             e_sb = pair.tile([P, PACK, LQ], F32)
@@ -179,15 +182,15 @@ def tile_alignment_vector_pa_kernel(tc, query, context, matrix, smooth, out):
                     in_=lrelu[n][:, t, :],
                     func=ACT.Exp,
                     bias=-float(smooth),
-                    scale=exp_scales[:, n, t : t + 1],
+                    scale=exp_scale[n][:, t : t + 1],
                 )
             weights[n] = e_sb
 
         def sum_over_sources(n):
-            s_ps = two_psum.tile([P, LQ + 1], F32, name="sums_ps")
+            s_ps = one_psum.tile([P, LQ + P], F32, name="sums_ps")
             for t in range(PACK):
                 nc.tensor.matmul(
-                    out=s_ps[:, LQ : LQ + 1], lhsT=weights[n][:, t, :], rhs=ones[:], start=(t == 0), stop=(t == PACK - 1)
+                    out=s_ps[:, LQ : LQ + P], lhsT=weights[n][:, t, :], rhs=ones[:], start=(t == 0), stop=(t == PACK - 1)
                 )
             sums_ps[n] = s_ps
 
@@ -216,20 +219,20 @@ def tile_alignment_vector_pa_kernel(tc, query, context, matrix, smooth, out):
             p_grouped[n] = grouped
 
         def quantise_weights(n):
-            codes = pair.tile([P, LQ], U32, align_bytes=64, name="p_codes")
-            scales = pair.tile([P, LQ], U8, align_bytes=64, name="p_scales")
+            codes = whole.tile([P, LQ], U32, align_bytes=64, name="p_codes")
+            scales = whole.tile([P, LQ], U8, align_bytes=64, name="p_scales")
             nc.vector.quantize_mx(out=codes[:].bitcast(FP8X4), scales=scales[:], in_=p_grouped[n][:])
             p_codes[n], p_scales[n] = codes, scales
 
         def weighted_sum(n):
             for h in range(D_HALVES):
-                o_ps = four_psum.tile([P, N_MAX], F32, tag="bank")
+                o_ps = one_psum.tile([P, N_MAX], F32, name="out_ps%d" % h)
                 nc.tensor.matmul_mx(
                     out=o_ps[:],
                     lhsT=p_codes[n][:].bitcast(FP8X4),
                     lhsT_scale=p_scales[n][:],
-                    rhs=c_codes[n * D_HALVES + h][:].bitcast(FP8X4),
-                    rhs_scale=c_scales[n * D_HALVES + h][:],
+                    rhs=c_codes[n, h][:].bitcast(FP8X4),
+                    rhs_scale=c_scales[n, h][:],
                     start=True,
                     stop=True,
                 )
@@ -245,38 +248,31 @@ def tile_alignment_vector_pa_kernel(tc, query, context, matrix, smooth, out):
             if 0 <= n < B:
                 stage(n, *more)
 
-        def run_half(stage, half):
-            if half < B * D_HALVES:
-                stage(half)
-
         ctx.enter_context(tc.manual_schedule())
         for n in range(B):
             load(n)
         gate_queries(0)
-
-        for i in range(STEPS_1):
+        for i in range(2 * B + 2):
+            run(invert_sums, i - 4)
+            run(spread_sums, i - 4)
+            run(norm_over_queries, i - 2)
+            run(exponentials, i - 3)
             run(transpose_queries, i)
-            run(transpose_sources, i, 0)
             run(quantise_queries, i - 1)
             run(quantise_features, i - 1, 0)
             run(quantise_features, i - 1, 1)
             run(score_matmul, i - 1)
-            run_half(regroup_sources, i)
             run(gate_queries, i + 1)
+            run(normalise_weights, i - 4)
+            run(regroup_sources, i, 0)
+            run(regroup_sources, i - B, 1)
+            run(quantise_weights, i - 4)
+            run(invert_norm, i - 2)
+            run(quantise_sources, i, 0)
+            run(quantise_sources, i - B, 1)
             run(leaky_relu, i - 1)
+            run(transpose_sources, i, 0)
             run(transpose_sources, i, 1)
-            run_half(quantise_sources, i)
-            run(sum_squares, i - 1)
-        invert_norms()
-
-        for k in range(B + 2):
-            run(exponentials, k)
-            run(weighted_sum, k - 2)
-            run(invert_sums, k - 1)
-            run(spread_sums, k - 1)
-            run(sum_over_sources, k)
-            run_half(regroup_sources, STEPS_1 + k)
-            run(normalise_weights, k - 1)
-            run_half(quantise_sources, STEPS_1 + k)
-            run(quantise_weights, k - 1)
-            run(store_result, k - 2)
+            run(sum_over_sources, i - 3)
+            run(weighted_sum, i - B - 1)
+            run(store_result, i - B - 1)

@@ -32,7 +32,7 @@ def tile_alignment_vector_pa_kernel(tc, query, context, matrix, smooth, out):
         pair = ctx.enter_context(tc.tile_pool(name="pair", bufs=2))
         kept = ctx.enter_context(tc.tile_pool(name="kept", bufs=4))
         whole = ctx.enter_context(tc.tile_pool(name="whole", bufs=B))
-        flip_psum = ctx.enter_context(tc.psum_pool(name="flip_psum", bufs=4))
+        flip_psum = ctx.enter_context(tc.psum_pool(name="flip_psum", bufs=6))
         one_psum = ctx.enter_context(tc.psum_pool(name="one_psum", bufs=1))
 
         ident_f32 = const.tile([P, P], F32)
@@ -226,7 +226,7 @@ def tile_alignment_vector_pa_kernel(tc, query, context, matrix, smooth, out):
 
         def weighted_sum(n):
             for h in range(D_HALVES):
-                o_ps = one_psum.tile([P, N_MAX], F32, name="out_ps%d" % h)
+                o_ps = flip_psum.tile([P, N_MAX], F32, tag="flip")
                 nc.tensor.matmul_mx(
                     out=o_ps[:],
                     lhsT=p_codes[n][:].bitcast(FP8X4),
@@ -252,27 +252,27 @@ def tile_alignment_vector_pa_kernel(tc, query, context, matrix, smooth, out):
         for n in range(B):
             load(n)
         gate_queries(0)
-        for i in range(2 * B + 2):
-            run(invert_sums, i - 4)
-            run(spread_sums, i - 4)
+        for i in range(B + 6):
             run(norm_over_queries, i - 2)
             run(exponentials, i - 3)
             run(transpose_queries, i)
+            run(transpose_sources, i, 0)
             run(quantise_queries, i - 1)
             run(quantise_features, i - 1, 0)
             run(quantise_features, i - 1, 1)
             run(score_matmul, i - 1)
+            run(invert_sums, i - 4)
+            run(spread_sums, i - 4)
             run(gate_queries, i + 1)
-            run(normalise_weights, i - 4)
             run(regroup_sources, i, 0)
-            run(regroup_sources, i - B, 1)
-            run(quantise_weights, i - 4)
+            run(regroup_sources, i - 5, 1)
+            run(normalise_weights, i - 4)
             run(invert_norm, i - 2)
             run(quantise_sources, i, 0)
-            run(quantise_sources, i - B, 1)
+            run(quantise_sources, i - 5, 1)
+            run(quantise_weights, i - 4)
             run(leaky_relu, i - 1)
-            run(transpose_sources, i, 0)
+            run(weighted_sum, i - 6)
+            run(store_result, i - 6)
             run(transpose_sources, i, 1)
             run(sum_over_sources, i - 3)
-            run(weighted_sum, i - B - 1)
-            run(store_result, i - B - 1)

@@ -39,7 +39,7 @@ def tile_alignment_vector_pa_kernel(tc, query, context, matrix, smooth, out):
         make_identity(nc, ident_f32[:])
         ident_bf16 = const.tile([P, P], BF16)
         make_identity(nc, ident_bf16[:])
-        ones = const.tile([P, P], F32)
+        ones = const.tile([P, 1], F32)
         nc.vector.memset(ones[:], 1.0)
         half = const.tile([P, PACK], F32)
         nc.vector.memset(half[:], 0.5)
@@ -187,10 +187,10 @@ def tile_alignment_vector_pa_kernel(tc, query, context, matrix, smooth, out):
             weights[n] = e_sb
 
         def sum_over_sources(n):
-            s_ps = one_psum.tile([P, LQ + P], F32, name="sums_ps")
+            s_ps = one_psum.tile([P, LQ + 1], F32, name="sums_ps")
             for t in range(PACK):
                 nc.tensor.matmul(
-                    out=s_ps[:, LQ : LQ + P], lhsT=weights[n][:, t, :], rhs=ones[:], start=(t == 0), stop=(t == PACK - 1)
+                    out=s_ps[:, LQ : LQ + 1], lhsT=weights[n][:, t, :], rhs=ones[:], start=(t == 0), stop=(t == PACK - 1)
                 )
             sums_ps[n] = s_ps
 

@@ -252,7 +252,7 @@ def tile_alignment_vector_pa_kernel(tc, query, context, matrix, smooth, out):
         for n in range(B):
             load(n)
         gate_queries(0)
-        for i in range(B + 6):
+        for i in range(B + 5):
             run(norm_over_queries, i - 2)
             run(exponentials, i - 3)
             run(transpose_queries, i)
@@ -265,14 +265,14 @@ def tile_alignment_vector_pa_kernel(tc, query, context, matrix, smooth, out):
             run(spread_sums, i - 4)
             run(gate_queries, i + 1)
             run(regroup_sources, i, 0)
-            run(regroup_sources, i - 5, 1)
+            run(regroup_sources, i - 3, 1)
             run(normalise_weights, i - 4)
             run(invert_norm, i - 2)
             run(quantise_sources, i, 0)
-            run(quantise_sources, i - 5, 1)
+            run(quantise_sources, i - 3, 1)
             run(quantise_weights, i - 4)
             run(leaky_relu, i - 1)
-            run(weighted_sum, i - 6)
-            run(store_result, i - 6)
+            run(weighted_sum, i - 5)
+            run(store_result, i - 5)
             run(transpose_sources, i, 1)
             run(sum_over_sources, i - 3)

from contextlib import ExitStack

import concourse.mybir as mybir
from concourse.masks import make_identity

FP8X4 = mybir.dt.float8_e4m3fn_x4
BF16 = mybir.dt.bfloat16
F32 = mybir.dt.float32
U32 = mybir.dt.uint32
U8 = mybir.dt.uint8
ACT = mybir.ActivationFunctionType
ALU = mybir.AluOpType

B, LQ, LS, D = 8, 128, 512, 1024
EPS = 1e-08
NEGATIVE_SLOPE = 0.1
P = 128
PACK = 4
K_PASS = P * PACK
D_PASSES = D // K_PASS
N_MAX = 512
D_HALVES = D // N_MAX
FLOPS = 2 * 2 * B * LS * LQ * D


def tile_alignment_vector_pa_kernel(tc, query, context, matrix, smooth, out):
    nc = tc.nc
    assert smooth > 0
    with ExitStack() as ctx:
        const = ctx.enter_context(tc.tile_pool(name="const", bufs=1))
        inputs = ctx.enter_context(tc.tile_pool(name="inputs", bufs=B))
        pair = ctx.enter_context(tc.tile_pool(name="pair", bufs=2))
        kept = ctx.enter_context(tc.tile_pool(name="kept", bufs=4))
        whole = ctx.enter_context(tc.tile_pool(name="whole", bufs=B))
        flip_psum = ctx.enter_context(tc.psum_pool(name="flip_psum", bufs=6))
        one_psum = ctx.enter_context(tc.psum_pool(name="one_psum", bufs=1))

        ident_f32 = const.tile([P, P], F32)
        make_identity(nc, ident_f32[:])
        ident_bf16 = const.tile([P, P], BF16)
        make_identity(nc, ident_bf16[:])
        ones = const.tile([P, 1], F32)
        nc.vector.memset(ones[:], 1.0)
        half = const.tile([P, PACK], F32)
        nc.vector.memset(half[:], 0.5)
        warm = const.tile([P, 1], F32)
        nc.scalar.activation(out=warm[:], in_=ones[:, 0:1], func=ACT.Exp)

        query_sb, matrix_sb, c_sb = {}, {}, {}
        q_sb, q_grouped, q_codes, q_scales = {}, {}, {}, {}
        ct_grouped, ct_codes, ct_scales = {}, {}, {}
        c_grouped, c_codes, c_scales = {}, {}, {}
        scores_ps, lrelu, norms, exp_scale, weights, sums_ps, sum_recip = {}, {}, {}, {}, {}, {}, {}
        p_grouped, p_codes, p_scales, out_ps = {}, {}, {}, {}

        def load(n):
            query_tile = inputs.tile([P, D], BF16)
            nc.sync.dma_start(out=query_tile[:], in_=query[n])
            matrix_tile = inputs.tile([P, D], BF16)
            nc.sync.dma_start(out=matrix_tile[:], in_=matrix[n])
            c_tile = inputs.tile([P, PACK, D], BF16)
            nc.sync.dma_start(out=c_tile[:], in_=context[n].rearrange("(p t) d -> p t d", t=PACK))
            query_sb[n], matrix_sb[n], c_sb[n] = query_tile, matrix_tile, c_tile

        def gate_queries(n):
            q_tile = pair.tile([P, D], BF16)
            nc.vector.tensor_tensor(out=q_tile[:], in0=query_sb[n][:], in1=matrix_sb[n][:], op=ALU.mult)
            q_sb[n] = q_tile

        def transpose_queries(n):
            by_parity = q_sb[n][:].rearrange("j (k r e) -> j k e r", r=P, e=2)
            qt_ps = flip_psum.tile([P, D_PASSES * PACK, LQ], BF16, tag="flip")
            for k in range(D // (2 * P)):
                for e in range(2):
                    nc.tensor.transpose(qt_ps[:, 2 * k + e, :], by_parity[:, k, e, :], ident_bf16[:])
            grouped = pair.tile([P, D_PASSES * LQ * PACK], BF16, align_bytes=64, name="q_grouped")
            nc.scalar.copy(
                out=grouped[:].rearrange("r (g j v) -> r g j v", g=D_PASSES, v=PACK),
                in_=qt_ps[:].rearrange("r (g v) j -> r g j v", g=D_PASSES),
            )
            q_grouped[n] = grouped

        def transpose_sources(n, g):
            grouped = pair.tile([P, PACK * P * PACK], BF16, align_bytes=64, name="ct_grouped%d" % g)
            grouped_words = grouped[:].bitcast(F32)
            for t_pair in range(PACK // 2):
                ct_ps = flip_psum.tile([P, 2, 2, P], F32, tag="flip")
                for x in range(2):
                    c_words = c_sb[n][:, 2 * t_pair + x, :].bitcast(F32)
                    for u in range(2):
                        k = 2 * g + u
                        nc.tensor.transpose(ct_ps[:, x, u, :], c_words[:, k * P : (k + 1) * P], ident_f32[:])
                nc.scalar.copy(
                    out=grouped_words[:, t_pair * N_MAX : (t_pair + 1) * N_MAX].rearrange(
                        "r (x p u) -> r x p u", x=2, u=2
                    ),
                    in_=ct_ps[:].rearrange("r x u p -> r x p u"),
                )
            ct_grouped[n, g] = grouped

        def quantise_queries(n):
            codes = pair.tile([P, D_PASSES * LQ], U32, align_bytes=64, name="q_codes")
            scales = pair.tile([P, D_PASSES * LQ], U8, align_bytes=64, name="q_scales")
            nc.vector.quantize_mx(out=codes[:].bitcast(FP8X4), scales=scales[:], in_=q_grouped[n][:])
            q_codes[n], q_scales[n] = codes, scales

        def quantise_features(n, g):
            codes = pair.tile([P, PACK * P], U32, align_bytes=64, name="ct_codes%d" % g)
            scales = pair.tile([P, PACK * P], U8, align_bytes=64, name="ct_scales%d" % g)
            nc.vector.quantize_mx(out=codes[:].bitcast(FP8X4), scales=scales[:], in_=ct_grouped[n, g][:])
            ct_codes[n, g], ct_scales[n, g] = codes, scales

        def regroup_sources(n, h):
            grouped = pair.tile([P, N_MAX, PACK], BF16, align_bytes=64, name="c_grouped%d" % h)
            nc.vector.tensor_copy(
                out=grouped[:].rearrange("p (c i) t -> p c t i", i=4),
                in_=c_sb[n][:, :, h * N_MAX : (h + 1) * N_MAX].rearrange("p t (c i) -> p c t i", i=4),
            )
            c_grouped[n, h] = grouped

        def quantise_sources(n, h):
            codes = whole.tile([P, N_MAX], U32, align_bytes=64, name="c_codes%d" % h)
            scales = whole.tile([P, N_MAX], U8, align_bytes=64, name="c_scales%d" % h)
            nc.vector.quantize_mx(
                out=codes[:].bitcast(FP8X4), scales=scales[:], in_=c_grouped[n, h][:].rearrange("p d t -> p (d t)")
            )
            c_codes[n, h], c_scales[n, h] = codes, scales

        def score_matmul(n):
            a_ps = one_psum.tile([P, PACK, LQ], F32, name="scores_ps")
            for t in range(PACK):
                for g in range(D_PASSES):
                    s_cols = slice(t * P, (t + 1) * P)
                    j_cols = slice(g * LQ, (g + 1) * LQ)
                    nc.tensor.matmul_mx(
                        out=a_ps[:, t, :],
                        lhsT=ct_codes[n, g][:, s_cols].bitcast(FP8X4),
                        lhsT_scale=ct_scales[n, g][:, s_cols],
                        rhs=q_codes[n][:, j_cols].bitcast(FP8X4),
                        rhs_scale=q_scales[n][:, j_cols],
                        start=(g == 0),
                        stop=(g == D_PASSES - 1),
                    )
            scores_ps[n] = a_ps

        def leaky_relu(n):
            a_sb = pair.tile([P, PACK, LQ], F32)
            nc.scalar.copy(out=a_sb[:], in_=scores_ps[n][:])
            l_sb = kept.tile([P, PACK, LQ], F32)
            nc.vector.scalar_tensor_tensor(
                out=l_sb[:], in0=a_sb[:], scalar=NEGATIVE_SLOPE, in1=a_sb[:], op0=ALU.mult, op1=ALU.max
            )
            lrelu[n] = l_sb

        def norm_over_queries(n):
            squares = pair.tile([P, LQ], F32)
            square_sum = pair.tile([P, PACK], F32)
            for t in range(PACK):
                nc.scalar.activation(
                    out=squares[:],
                    in_=lrelu[n][:, t, :],
                    func=ACT.Square,
                    scale=1.0 / smooth,
                    accum_out=square_sum[:, t : t + 1],
                )
            root = pair.tile([P, PACK], F32)
            nc.gpsimd.tensor_tensor(out=root[:], in0=square_sum[:], in1=half[:], op=ALU.pow)
            norm = pair.tile([P, PACK], F32)
            nc.gpsimd.tensor_scalar(out=norm[:], in0=root[:], scalar1=EPS / smooth, scalar2=None, op0=ALU.add)
            norms[n] = norm

        def invert_norm(n):
            scale = pair.tile([P, PACK], F32)
            nc.vector.reciprocal(out=scale[:], in_=norms[n][:])
            exp_scale[n] = scale

        def exponentials(n):
            e_sb = pair.tile([P, PACK, LQ], F32)
            for t in range(PACK):
                nc.scalar.activation(
                    out=e_sb[:, t, :],
                    in_=lrelu[n][:, t, :],
                    func=ACT.Exp,
                    bias=-float(smooth),
                    scale=exp_scale[n][:, t : t + 1],
                )
            weights[n] = e_sb

        def sum_over_sources(n):
            s_ps = one_psum.tile([P, LQ + 1], F32, name="sums_ps")
            for t in range(PACK):
                nc.tensor.matmul(
                    out=s_ps[:, LQ : LQ + 1], lhsT=weights[n][:, t, :], rhs=ones[:], start=(t == 0), stop=(t == PACK - 1)
                )
            sums_ps[n] = s_ps

        def invert_sums(n):
            recip = pair.tile([P, 1], F32)
            nc.vector.reciprocal(out=recip[:], in_=sums_ps[n][:, LQ : LQ + 1])
            sum_recip[n] = recip

        def spread_sums(n):
            nc.tensor.matmul(
                out=sums_ps[n][:, 0:LQ],
                lhsT=sum_recip[n][:, 0:1].to_broadcast([P, P]),
                rhs=ident_f32[:],
                start=True,
                stop=True,
            )

        def normalise_weights(n):
            grouped = pair.tile([P, LQ * PACK], BF16, align_bytes=64, name="p_grouped")
            nc.vector.tensor_tensor(
                out=grouped[:].rearrange("p (j t) -> p j t", t=PACK),
                in0=weights[n][:].rearrange("p t j -> p j t"),
                in1=sums_ps[n][:, 0:LQ].unsqueeze(2).to_broadcast([P, LQ, PACK]),
                op=ALU.mult,
            )
            p_grouped[n] = grouped

        def quantise_weights(n):
            codes = whole.tile([P, LQ], U32, align_bytes=64, name="p_codes")
            scales = whole.tile([P, LQ], U8, align_bytes=64, name="p_scales")
            nc.vector.quantize_mx(out=codes[:].bitcast(FP8X4), scales=scales[:], in_=p_grouped[n][:])
            p_codes[n], p_scales[n] = codes, scales

        def weighted_sum(n):
            for h in range(D_HALVES):
                o_ps = flip_psum.tile([P, N_MAX], F32, tag="flip")
                nc.tensor.matmul_mx(
                    out=o_ps[:],
                    lhsT=p_codes[n][:].bitcast(FP8X4),
                    lhsT_scale=p_scales[n][:],
                    rhs=c_codes[n, h][:].bitcast(FP8X4),
                    rhs_scale=c_scales[n, h][:],
                    start=True,
                    stop=True,
                )
                out_ps[n, h] = o_ps

        def store_result(n):
            for h in range(D_HALVES):
                out_sb = pair.tile([P, N_MAX], F32, name="out_sb%d" % h)
                nc.scalar.copy(out=out_sb[:], in_=out_ps[n, h][:])
                nc.sync.dma_start(out=out[n][:, h * N_MAX : (h + 1) * N_MAX], in_=out_sb[:])

        def run(stage, n, *more):
            if 0 <= n < B:
                stage(n, *more)

        ctx.enter_context(tc.manual_schedule())
        for n in range(B):
            load(n)
        gate_queries(0)
        for i in range(B + 5):
            run(norm_over_queries, i - 2)
            run(exponentials, i - 3)
            run(transpose_queries, i)
            run(transpose_sources, i, 0)
            run(quantise_queries, i - 1)
            run(quantise_features, i - 1, 0)
            run(quantise_features, i - 1, 1)
            run(score_matmul, i - 1)
            run(invert_sums, i - 4)
            run(spread_sums, i - 4)
            run(gate_queries, i + 1)
            run(regroup_sources, i, 0)
            run(regroup_sources, i - 3, 1)
            run(normalise_weights, i - 4)
            run(invert_norm, i - 2)
            run(quantise_sources, i, 0)
            run(quantise_sources, i - 3, 1)
            run(quantise_weights, i - 4)
            run(leaky_relu, i - 1)
            run(weighted_sum, i - 5)
            run(store_result, i - 5)
            run(transpose_sources, i, 1)
            run(sum_over_sources, i - 3)
